import numpy as np
import ml_dtypes


def mxq(x, axis, fmt="e4m3"):
    dtype, down = {"e4m3": (ml_dtypes.float8_e4m3fn, 7), "e5m2": (ml_dtypes.float8_e5m2, 14)}[fmt]
    v = np.moveaxis(np.asarray(x, np.float32).astype(ml_dtypes.bfloat16).astype(np.float64), axis, -1)
    blocks = v.reshape(v.shape[:-1] + (-1, 32))
    amax = np.abs(blocks).max(-1, keepdims=True)
    byte = np.maximum(np.where(amax > 0, np.frexp(amax)[1] - 1 + 127, 0) - down, 1)
    scale = np.exp2(byte - 127.0)
    codes = (blocks / scale).astype(np.float32).astype(dtype).astype(np.float64)
    return np.moveaxis((codes * scale).reshape(v.shape), -1, axis)


WIDE = False


def mx_kscale(k):
    if not WIDE:
        return np.ones(k)
    levels = np.array([10, -10, 5, -5, 0])
    a = np.random.permutation(np.resize(levels, k // 512 * 4)).reshape(k // 512, 4)
    idx = np.arange(k)
    return np.exp2(a[idx // 512, idx % 128 // 32])


BF16 = ml_dtypes.bfloat16


def bf(x):
    return np.asarray(x, np.float32).astype(BF16)


def f64(x):
    return np.asarray(x).astype(np.float64)


E2M1 = np.array([0.0, 0.5, 1.0, 1.5, 2.0, 3.0, 4.0, 6.0, -0.0, -0.5, -1.0, -1.5, -2.0, -3.0, -4.0, -6.0])


def pack_weight(w, fmt):
    k, n = w.shape
    w = f64(bf(w)).reshape(k // 32, 32, n)
    amax = np.abs(w).max(1)
    if fmt == "e4m3":
        byte = np.frexp(amax)[1] - 1 + 127 - 7
    else:
        mant, ex = np.frexp(amax / 6.0)
        byte = np.where(mant > 0.5, ex, ex - 1) + 127
    byte = np.clip(np.where(amax > 0, byte, 1), 1, 254)
    scaled = (w * np.exp2(127.0 - byte)[:, None, :]).reshape(k, n).astype(np.float32)
    by_word = np.ascontiguousarray(scaled.reshape(k // 512, 128, 4, n).transpose(0, 1, 3, 2))
    if fmt == "e4m3":
        words = by_word.astype(ml_dtypes.float8_e4m3fn).view(np.uint8)
    else:
        c = by_word.astype(ml_dtypes.float4_e2m1fn).view(np.uint8) & 0xF
        words = c[..., 0::2] | (c[..., 1::2] << 4)
    return np.ascontiguousarray(words), np.ascontiguousarray(byte.astype(np.uint8).reshape(k // 512, 16, n))


def unpack_weight(words, scales, fmt):
    g, p, n, _ = words.shape
    if fmt == "e4m3":
        vals = np.ascontiguousarray(words).view(ml_dtypes.float8_e4m3fn).astype(np.float64)
    else:
        nib = np.empty((g, p, n, 4), np.uint8)
        nib[..., 0::2] = words & 0xF
        nib[..., 1::2] = words >> 4
        vals = E2M1[nib]
    vals = vals * np.repeat(np.exp2(scales.astype(np.float64) - 127.0), 8, axis=1)[..., None]
    return vals.transpose(0, 1, 3, 2).reshape(g * 512, n)

def pack4(w):
    words, scales = pack_weight(w, "e2m1")
    return words.reshape(words.shape[0], 128, -1), scales


def unpack4(words, scales):
    return unpack_weight(words.reshape(words.shape[0], 128, -1, 2), scales, "e2m1")


H, D_CONTENT, D_POS, D_K, D_V, B, L = 16, 512, 128, 128, 128, 8, 512
D_MODEL = D_CONTENT + D_POS
T = B * L
DV1 = D_V // 2
KP = H * DV1
EPS = 1e-3


def setup_inputs():
    s1, s2 = mx_kscale(KP), mx_kscale(KP)
    sc = np.concatenate([s1.reshape(H, DV1), s2.reshape(H, DV1)], axis=1)
    attn_out = bf(np.random.standard_normal((H, B, L, D_V)) * 0.4 * sc[:, None, None, :])
    inp = bf(np.random.standard_normal((T, D_MODEL)) * 0.05 + np.random.standard_normal((T, 1)) * 0.03)
    w_proj1_words, w_proj1_scales = pack4(np.random.standard_normal((KP, D_CONTENT)) * 0.1 / np.sqrt(KP) / s1[:, None])
    w_proj2_words, w_proj2_scales = pack4(np.random.standard_normal((KP, D_POS)) * 0.1 / np.sqrt(KP) / s2[:, None])
    ln_a = bf(1.0 + 0.1 * np.random.standard_normal(D_MODEL))
    ln_b = bf(0.1 * np.random.standard_normal(D_MODEL))
    return {
        "attn_out": attn_out,
        "inp": inp,
        "w_proj1_words": w_proj1_words,
        "w_proj1_scales": w_proj1_scales,
        "w_proj2_words": w_proj2_words,
        "w_proj2_scales": w_proj2_scales,
        "ln_a": ln_a,
        "ln_b": ln_b,
    }


def reference(attn_out, inp, w_proj1_words, w_proj1_scales, w_proj2_words, w_proj2_scales, ln_a, ln_b):
    o = f64(attn_out).reshape(H, T, D_V).transpose(1, 0, 2)
    o1 = o[:, :, :DV1].reshape(T, KP)
    o2 = o[:, :, DV1:].reshape(T, KP)
    y1 = mxq(o1, 1, "e4m3") @ unpack4(w_proj1_words, w_proj1_scales)
    y2 = mxq(o2, 1, "e4m3") @ unpack4(w_proj2_words, w_proj2_scales)
    z = np.concatenate([y1, y2], -1) + f64(inp)
    mu = np.mean(z, axis=-1, keepdims=True)
    sigma = np.std(z, axis=-1, keepdims=True, ddof=1)
    ln = (z - mu) / (sigma + EPS)
    return ln * f64(ln_a) + f64(ln_b)

@@ -1,0 +1,267 @@
+from contextlib import ExitStack
+
+import concourse.mybir as mybir
+from concourse.masks import make_identity
+
+F32 = mybir.dt.float32
+BF16 = mybir.dt.bfloat16
+I32 = mybir.dt.int32
+U32 = mybir.dt.uint32
+U8 = mybir.dt.uint8
+FP8X4 = mybir.dt.float8_e4m3fn_x4
+FP4X4 = mybir.dt.float4_e2m1fn_x4
+ALU = mybir.AluOpType
+ACT = mybir.ActivationFunctionType
+
+P = 128
+HEADS = 16
+D_HEAD = 128
+TOKENS = 4096
+N1 = 512
+N2 = 128
+N_OUT = N1 + N2
+EPS = 1e-3
+
+HALVES = 2
+PASSES = 2
+HEADS_PER_PASS = HEADS // PASSES
+QUADS = 16
+PAIRS = 2
+
+ROWS = 4
+CHUNK = P * ROWS
+N_CHUNKS = TOKENS // CHUNK
+N_TILES = TOKENS // P
+
+VECTOR_SORTS_EVERY = 4
+
+FLOPS = 2 * TOKENS * (HEADS * 64) * N_OUT
+
+
+def tile_multiheadattention_pa_t_kernel(
+    tc, attn_out, inp, w_proj1_words, w_proj1_scales, w_proj2_words, w_proj2_scales, ln_a, ln_b, out
+):
+    nc = tc.nc
+    with ExitStack() as ctx:
+        const = ctx.enter_context(tc.tile_pool(name="const", bufs=1))
+        x_pool = ctx.enter_context(tc.tile_pool(name="x_pool", bufs=3))
+        inp_pool = ctx.enter_context(tc.tile_pool(name="inp_pool", bufs=5))
+        front = ctx.enter_context(tc.tile_pool(name="front", bufs=3))
+        back = ctx.enter_context(tc.tile_pool(name="back", bufs=4))
+        small = ctx.enter_context(tc.tile_pool(name="small", bufs=4))
+        tp_pool = ctx.enter_context(tc.psum_pool(name="tp_pool", bufs=4))
+        y_pool = ctx.enter_context(tc.psum_pool(name="y_pool", bufs=2))
+
+        x_view = attn_out.rearrange("h b l d -> h (b l) d")
+        inp_view = inp.rearrange("(c p i) n -> c p (i n)", p=P, i=ROWS)
+        out_view = out.rearrange("(c p i) n -> c p i n", p=P, i=ROWS)
+
+        x_tiles = {}
+        inp_tiles = {}
+
+        def load_chunk(c, row_by_row):
+            x_sb = x_pool.tile([P, HEADS, ROWS, D_HEAD], BF16, name="x_sb")
+            rows = x_view[:, c * CHUNK : (c + 1) * CHUNK, :].rearrange("h (p i) d -> p h i d", i=ROWS)
+            if row_by_row:
+                for i in range(ROWS):
+                    nc.sync.dma_start(out=x_sb[:, :, i, :], in_=rows[:, :, i, :])
+            else:
+                for g in range(PASSES):
+                    heads = slice(g * HEADS_PER_PASS, (g + 1) * HEADS_PER_PASS)
+                    nc.sync.dma_start(
+                        out=x_sb[:, heads].rearrange("p h i d -> p h (i d)"),
+                        in_=rows[:, heads].rearrange("p h i d -> p h (i d)"),
+                    )
+            x_tiles[c] = x_sb
+            inp_sb = inp_pool.tile([P, ROWS, N_OUT], BF16, name="inp_sb")
+            nc.sync.dma_start(out=inp_sb[:].rearrange("p i n -> p (i n)"), in_=inp_view[c])
+            inp_tiles[c] = inp_sb
+
+        load_chunk(0, row_by_row=True)
+
+        w1 = const.tile([P, PASSES * 2 * N1], U8, align_bytes=64)
+        w2 = const.tile([P, PASSES * 2 * N2], U8, align_bytes=64)
+        w1_scl = const.tile([P, PASSES * N1], U8, align_bytes=64)
+        w2_scl = const.tile([P, PASSES * N2], U8, align_bytes=64)
+        nc.vector.memset(w1_scl[:].bitcast(I32), 0)
+        nc.vector.memset(w2_scl[:].bitcast(I32), 0)
+        nc.sync.dma_start(
+            out=w1[:].bitcast(I32).rearrange("p (g n) -> p g n", g=PASSES),
+            in_=w_proj1_words.bitcast(I32).rearrange("g p n -> p g n"),
+        )
+        nc.sync.dma_start(
+            out=w2[:].bitcast(I32).rearrange("p (g n) -> p g n", g=PASSES),
+            in_=w_proj2_words.bitcast(I32).rearrange("g p n -> p g n"),
+        )
+        for quadrant in range(4):
+            for plane, scales in ((w1_scl, w_proj1_scales), (w2_scl, w_proj2_scales)):
+                nc.sync.dma_start(
+                    out=plane[32 * quadrant : 32 * quadrant + 4, :]
+                    .bitcast(I32)
+                    .rearrange("r (g n) -> r g n", g=PASSES),
+                    in_=scales[:, 4 * quadrant : 4 * quadrant + 4, :].bitcast(I32).rearrange("g r n -> r g n"),
+                )
+
+        gain = const.tile([P, N_OUT], BF16)
+        bias = const.tile([P, N_OUT], BF16)
+        nc.sync.dma_start(out=gain[:], in_=ln_a.partition_broadcast(P))
+        nc.sync.dma_start(out=bias[:], in_=ln_b.partition_broadcast(P))
+        load_chunk(1, row_by_row=False)
+
+        ident = const.tile([P, P], F32)
+        make_identity(nc, ident[:])
+        half = const.tile([P, 1], F32)
+        minus_one = const.tile([P, 1], F32)
+        nc.gpsimd.memset(half[:], 0.5)
+        nc.gpsimd.memset(minus_one[:], -1.0)
+
+        sorted_words = {}
+        transposed = {}
+        grouped = {}
+        codes = {}
+        code_scales = {}
+        y1 = {}
+        y2 = {}
+        z = {}
+        neg_mean = {}
+        centred = {}
+        inv_sigma = {}
+
+        def sort_words(k):
+            c, i = divmod(k, ROWS)
+            words = (
+                x_tiles[c][:]
+                .rearrange("p h i d -> p (h i d)")
+                .bitcast(F32)
+                .rearrange("p (h i s m u) -> p h i s m u", h=HEADS, i=ROWS, s=HALVES, m=QUADS, u=PAIRS)
+            )
+            y_sb = front.tile([P, HALVES, PAIRS, HEADS, QUADS], F32, name="y_sb")
+            for s in range(HALVES):
+                picked = words[:, :, i, s, :, :].rearrange("p h m u -> p u h m")
+                if s == 0 and k % VECTOR_SORTS_EVERY == 0:
+                    nc.vector.tensor_copy(out=y_sb[:, s], in_=picked)
+                else:
+                    nc.scalar.copy(out=y_sb[:, s], in_=picked)
+            sorted_words[k] = y_sb
+
+        def transpose_words(k):
+            y_sb = sorted_words.pop(k)
+            banks = []
+            for s in range(HALVES):
+                tp = tp_pool.tile([P, PASSES, PAIRS, P], F32, name="tp")
+                for g in range(PASSES):
+                    heads = slice(g * HEADS_PER_PASS, (g + 1) * HEADS_PER_PASS)
+                    for u in range(PAIRS):
+                        nc.tensor.transpose(
+                            tp[:, g, u, :], y_sb[:, s, u, heads, :].rearrange("p h m -> p (h m)"), ident[:]
+                        )
+                banks.append(tp)
+            transposed[k] = banks
+
+        def group_words(k):
+            banks = transposed.pop(k)
+            g_sb = front.tile([P, HALVES, PASSES * P * 4], BF16, name="g_sb", align_bytes=64)
+            for s in range(HALVES):
+                nc.scalar.copy(
+                    out=g_sb[:, s, :].bitcast(F32).rearrange("p (g t u) -> p g t u", g=PASSES, u=PAIRS),
+                    in_=banks[s][:].rearrange("p g u t -> p g t u"),
+                )
+            grouped[k] = g_sb
+
+        def quantise(k):
+            g_sb = grouped.pop(k)
+            c_sb = front.tile([P, HALVES * PASSES * P], U32, name="c_sb", align_bytes=64)
+            s_sb = front.tile([P, HALVES * PASSES * P], U8, name="s_sb", align_bytes=64)
+            nc.vector.quantize_mx(
+                out=c_sb[:].bitcast(FP8X4), scales=s_sb[:], in_=g_sb[:].rearrange("p s e -> p (s e)")
+            )
+            codes[k] = c_sb
+            code_scales[k] = s_sb
+
+        def project(k):
+            c_sb = codes.pop(k)
+            s_sb = code_scales.pop(k)
+            y1_ps = y_pool.tile([P, N1], F32, name="y1_ps")
+            y2_ps = y_pool.tile([P, N2], F32, name="y2_ps")
+            for s, (acc, w, w_scl, n) in enumerate(((y1_ps, w1, w1_scl, N1), (y2_ps, w2, w2_scl, N2))):
+                for g in range(PASSES):
+                    cols = slice((s * PASSES + g) * P, (s * PASSES + g + 1) * P)
+                    nc.tensor.matmul_mx(
+                        out=acc[:],
+                        lhsT=c_sb[:, cols].bitcast(FP8X4),
+                        lhsT_scale=s_sb[:, cols],
+                        rhs=w[:, g * 2 * n : (g + 1) * 2 * n].bitcast(FP4X4),
+                        rhs_scale=w_scl[:, g * n : (g + 1) * n],
+                        start=(g == 0),
+                        stop=(g == PASSES - 1),
+                    )
+            y1[k] = y1_ps
+            y2[k] = y2_ps
+
+        def add_residual(k):
+            c, i = divmod(k, ROWS)
+            z_sb = back.tile([P, N_OUT], F32, name="z_sb")
+            sums = small.tile([P, 2], F32, name="sums")
+            nc.vector.scalar_tensor_tensor(
+                out=z_sb[:, 0:N1], in0=y1.pop(k)[:], scalar=1.0, in1=inp_tiles[c][:, i, 0:N1],
+                op0=ALU.mult, op1=ALU.add, accum_out=sums[:, 0:1],
+            )
+            nc.vector.scalar_tensor_tensor(
+                out=z_sb[:, N1:N_OUT], in0=y2.pop(k)[:], scalar=1.0, in1=inp_tiles[c][:, i, N1:N_OUT],
+                op0=ALU.mult, op1=ALU.add, accum_out=sums[:, 1:2],
+            )
+            nm = small.tile([P, 1], F32, name="nm")
+            nc.gpsimd.tensor_scalar(
+                out=nm[:], in0=sums[:, 0:1], scalar1=sums[:, 1:2], scalar2=-1.0 / N_OUT, op0=ALU.add, op1=ALU.mult
+            )
+            z[k] = z_sb
+            neg_mean[k] = nm
+
+        def centre(k):
+            z_sb = z.pop(k)
+            nm = neg_mean.pop(k)
+            squares = back.tile([P, N_OUT], BF16, name="squares")
+            ssq = small.tile([P, 1], F32, name="ssq")
+            nc.scalar.activation(
+                out=squares[:], in_=z_sb[:], func=ACT.Square, bias=nm[:, 0:1], scale=1.0, accum_out=ssq[:, 0:1]
+            )
+            c_sb = back.tile([P, N_OUT], F32, name="cen_sb")
+            nc.vector.scalar_tensor_tensor(
+                out=c_sb[:], in0=z_sb[:], scalar=nm[:, 0:1], in1=gain[:], op0=ALU.add, op1=ALU.mult
+            )
+            root = small.tile([P, 1], F32, name="root")
+            sigma_eps = small.tile([P, 1], F32, name="sigma_eps")
+            inv = small.tile([P, 1], F32, name="inv")
+            nc.gpsimd.tensor_tensor(out=root[:], in0=ssq[:], in1=half[:], op=ALU.pow)
+            nc.gpsimd.tensor_scalar(
+                out=sigma_eps[:], in0=root[:], scalar1=(N_OUT - 1) ** -0.5, scalar2=EPS, op0=ALU.mult, op1=ALU.add
+            )
+            nc.gpsimd.tensor_tensor(out=inv[:], in0=sigma_eps[:], in1=minus_one[:], op=ALU.pow)
+            centred[k] = c_sb
+            inv_sigma[k] = inv
+
+        def finish(k):
+            c, i = divmod(k, ROWS)
+            o_sb = back.tile([P, N_OUT], F32, name="o_sb")
+            nc.vector.scalar_tensor_tensor(
+                out=o_sb[:], in0=centred.pop(k)[:], scalar=inv_sigma.pop(k)[:, 0:1], in1=bias[:],
+                op0=ALU.mult, op1=ALU.add,
+            )
+            nc.sync.dma_start(out=out_view[c][:, i, :], in_=o_sb[:])
+
+        def run(stage, k):
+            if 0 <= k < N_TILES:
+                stage(k)
+
+        with tc.manual_schedule():
+            for step in range(N_TILES + 8):
+                if step % ROWS == 0 and step // ROWS + 2 < N_CHUNKS:
+                    load_chunk(step // ROWS + 2, row_by_row=False)
+                run(project, step - 4)
+                run(add_residual, step - 5)
+                run(transpose_words, step - 1)
+                run(group_words, step - 2)
+                run(quantise, step - 3)
+                run(centre, step - 6)
+                run(finish, step - 7)
+                run(sort_words, step)

@@ -59,25 +59,18 @@ def tile_multiheadattention_pa_t_kernel(
         x_tiles = {}
         inp_tiles = {}
 
-        def load_chunk(c, row_by_row):
+        def load_chunk(c):
             x_sb = x_pool.tile([P, HEADS, ROWS, D_HEAD], BF16, name="x_sb")
-            rows = x_view[:, c * CHUNK : (c + 1) * CHUNK, :].rearrange("h (p i) d -> p h i d", i=ROWS)
-            if row_by_row:
-                for i in range(ROWS):
-                    nc.sync.dma_start(out=x_sb[:, :, i, :], in_=rows[:, :, i, :])
-            else:
-                for g in range(PASSES):
-                    heads = slice(g * HEADS_PER_PASS, (g + 1) * HEADS_PER_PASS)
-                    nc.sync.dma_start(
-                        out=x_sb[:, heads].rearrange("p h i d -> p h (i d)"),
-                        in_=rows[:, heads].rearrange("p h i d -> p h (i d)"),
-                    )
+            rows = x_view[:, c * CHUNK : (c + 1) * CHUNK, :].rearrange("h (p i) d -> p h (i d)", i=ROWS)
+            for g in range(PASSES):
+                heads = slice(g * HEADS_PER_PASS, (g + 1) * HEADS_PER_PASS)
+                nc.sync.dma_start(out=x_sb[:, heads].rearrange("p h i d -> p h (i d)"), in_=rows[:, heads, :])
             x_tiles[c] = x_sb
             inp_sb = inp_pool.tile([P, ROWS, N_OUT], BF16, name="inp_sb")
             nc.sync.dma_start(out=inp_sb[:].rearrange("p i n -> p (i n)"), in_=inp_view[c])
             inp_tiles[c] = inp_sb
 
-        load_chunk(0, row_by_row=True)
+        load_chunk(0)
 
         w1 = const.tile([P, PASSES * 2 * N1], U8, align_bytes=64)
         w2 = const.tile([P, PASSES * 2 * N2], U8, align_bytes=64)
@@ -106,14 +99,13 @@ def tile_multiheadattention_pa_t_kernel(
         bias = const.tile([P, N_OUT], BF16)
         nc.sync.dma_start(out=gain[:], in_=ln_a.partition_broadcast(P))
         nc.sync.dma_start(out=bias[:], in_=ln_b.partition_broadcast(P))
-        load_chunk(1, row_by_row=False)
+        load_chunk(1)
 
         ident = const.tile([P, P], F32)
         make_identity(nc, ident[:])
-        half = const.tile([P, 1], F32)
-        minus_one = const.tile([P, 1], F32)
-        nc.gpsimd.memset(half[:], 0.5)
-        nc.gpsimd.memset(minus_one[:], -1.0)
+        one = const.tile([P, 1], F32)
+        nc.vector.memset(one[:], 1.0)
+        nc.scalar.activation(out=one[:], in_=one[:], func=ACT.Sqrt)
 
         sorted_words = {}
         transposed = {}
@@ -123,7 +115,10 @@ def tile_multiheadattention_pa_t_kernel(
         y1 = {}
         y2 = {}
         z = {}
+        row_sums = {}
         neg_mean = {}
+        square_sums = {}
+        sigma = {}
         centred = {}
         inv_sigma = {}
 
@@ -210,34 +205,43 @@ def tile_multiheadattention_pa_t_kernel(
                 out=z_sb[:, N1:N_OUT], in0=y2.pop(k)[:], scalar=1.0, in1=inp_tiles[c][:, i, N1:N_OUT],
                 op0=ALU.mult, op1=ALU.add, accum_out=sums[:, 1:2],
             )
+            z[k] = z_sb
+            row_sums[k] = sums
+
+        def negate_mean(k):
+            sums = row_sums.pop(k)
             nm = small.tile([P, 1], F32, name="nm")
-            nc.gpsimd.tensor_scalar(
+            nc.vector.tensor_scalar(
                 out=nm[:], in0=sums[:, 0:1], scalar1=sums[:, 1:2], scalar2=-1.0 / N_OUT, op0=ALU.add, op1=ALU.mult
             )
-            z[k] = z_sb
             neg_mean[k] = nm
 
-        def centre(k):
-            z_sb = z.pop(k)
-            nm = neg_mean.pop(k)
+        def sum_squares(k):
             squares = back.tile([P, N_OUT], BF16, name="squares")
             ssq = small.tile([P, 1], F32, name="ssq")
             nc.scalar.activation(
-                out=squares[:], in_=z_sb[:], func=ACT.Square, bias=nm[:, 0:1], scale=1.0, accum_out=ssq[:, 0:1]
+                out=squares[:], in_=z[k][:], func=ACT.Square, bias=neg_mean[k][:, 0:1], scale=1.0,
+                accum_out=ssq[:, 0:1],
             )
+            square_sums[k] = ssq
+
+        def centre(k):
             c_sb = back.tile([P, N_OUT], F32, name="cen_sb")
             nc.vector.scalar_tensor_tensor(
-                out=c_sb[:], in0=z_sb[:], scalar=nm[:, 0:1], in1=gain[:], op0=ALU.add, op1=ALU.mult
+                out=c_sb[:], in0=z.pop(k)[:], scalar=neg_mean.pop(k)[:, 0:1], in1=gain[:], op0=ALU.add, op1=ALU.mult
             )
-            root = small.tile([P, 1], F32, name="root")
+            centred[k] = c_sb
+
+        def root(k):
+            sg = small.tile([P, 1], F32, name="sg")
+            nc.scalar.activation(out=sg[:], in_=square_sums.pop(k)[:], func=ACT.Sqrt, scale=1.0 / (N_OUT - 1))
+            sigma[k] = sg
+
+        def invert_sigma(k):
             sigma_eps = small.tile([P, 1], F32, name="sigma_eps")
             inv = small.tile([P, 1], F32, name="inv")
-            nc.gpsimd.tensor_tensor(out=root[:], in0=ssq[:], in1=half[:], op=ALU.pow)
-            nc.gpsimd.tensor_scalar(
-                out=sigma_eps[:], in0=root[:], scalar1=(N_OUT - 1) ** -0.5, scalar2=EPS, op0=ALU.mult, op1=ALU.add
-            )
-            nc.gpsimd.tensor_tensor(out=inv[:], in0=sigma_eps[:], in1=minus_one[:], op=ALU.pow)
-            centred[k] = c_sb
+            nc.vector.tensor_scalar_add(out=sigma_eps[:], in0=sigma.pop(k)[:], scalar1=EPS)
+            nc.vector.reciprocal(out=inv[:], in_=sigma_eps[:])
             inv_sigma[k] = inv
 
         def finish(k):
@@ -256,12 +260,16 @@ def tile_multiheadattention_pa_t_kernel(
         with tc.manual_schedule():
             for step in range(N_TILES + 8):
                 if step % ROWS == 0 and step // ROWS + 2 < N_CHUNKS:
-                    load_chunk(step // ROWS + 2, row_by_row=False)
+                    load_chunk(step // ROWS + 2)
                 run(project, step - 4)
                 run(add_residual, step - 5)
                 run(transpose_words, step - 1)
                 run(group_words, step - 2)
                 run(quantise, step - 3)
+                run(negate_mean, step - 5)
+                run(sum_squares, step - 6)
                 run(centre, step - 6)
+                run(invert_sigma, step - 7)
                 run(finish, step - 7)
                 run(sort_words, step)
+                run(root, step - 6)

@@ -119,6 +119,7 @@ def tile_multiheadattention_pa_t_kernel(
         neg_mean = {}
         square_sums = {}
         sigma = {}
+        sigma_eps = {}
         centred = {}
         inv_sigma = {}
 
@@ -237,11 +238,14 @@ def tile_multiheadattention_pa_t_kernel(
             nc.scalar.activation(out=sg[:], in_=square_sums.pop(k)[:], func=ACT.Sqrt, scale=1.0 / (N_OUT - 1))
             sigma[k] = sg
 
-        def invert_sigma(k):
-            sigma_eps = small.tile([P, 1], F32, name="sigma_eps")
+        def add_eps(k):
+            se = small.tile([P, 1], F32, name="se")
+            nc.vector.tensor_scalar_add(out=se[:], in0=sigma.pop(k)[:], scalar1=EPS)
+            sigma_eps[k] = se
+
+        def invert(k):
             inv = small.tile([P, 1], F32, name="inv")
-            nc.vector.tensor_scalar_add(out=sigma_eps[:], in0=sigma.pop(k)[:], scalar1=EPS)
-            nc.vector.reciprocal(out=inv[:], in_=sigma_eps[:])
+            nc.vector.reciprocal(out=inv[:], in_=sigma_eps.pop(k)[:])
             inv_sigma[k] = inv
 
         def finish(k):
@@ -265,11 +269,12 @@ def tile_multiheadattention_pa_t_kernel(
                 run(add_residual, step - 5)
                 run(transpose_words, step - 1)
                 run(group_words, step - 2)
+                run(add_eps, step - 7)
                 run(quantise, step - 3)
-                run(negate_mean, step - 5)
+                run(invert, step - 7)
                 run(sum_squares, step - 6)
                 run(centre, step - 6)
-                run(invert_sigma, step - 7)
+                run(negate_mean, step - 5)
                 run(finish, step - 7)
                 run(sort_words, step)
                 run(root, step - 6)

@@ -33,8 +33,6 @@ CHUNK = P * ROWS
 N_CHUNKS = TOKENS // CHUNK
 N_TILES = TOKENS // P
 
-VECTOR_SORTS_EVERY = 4
-
 FLOPS = 2 * TOKENS * (HEADS * 64) * N_OUT
 
 
@@ -134,7 +132,7 @@ def tile_multiheadattention_pa_t_kernel(
             y_sb = front.tile([P, HALVES, PAIRS, HEADS, QUADS], F32, name="y_sb")
             for s in range(HALVES):
                 picked = words[:, :, i, s, :, :].rearrange("p h m u -> p u h m")
-                if s == 0 and k % VECTOR_SORTS_EVERY == 0:
+                if s == 0:
                     nc.vector.tensor_copy(out=y_sb[:, s], in_=picked)
                 else:
                     nc.scalar.copy(out=y_sb[:, s], in_=picked)

@@ -21,6 +21,8 @@ N1 = 512
 N2 = 128
 N_OUT = N1 + N2
 EPS = 1e-3
+BANK = 512
+SPREAD_STEP = 2
 
 HALVES = 2
 PASSES = 2
@@ -28,10 +30,12 @@ HEADS_PER_PASS = HEADS // PASSES
 QUADS = 16
 PAIRS = 2
 
-ROWS = 4
+ROWS = 2
 CHUNK = P * ROWS
 N_CHUNKS = TOKENS // CHUNK
 N_TILES = TOKENS // P
+
+VECTOR_SORTS_EVERY = 4
 
 FLOPS = 2 * TOKENS * (HEADS * 64) * N_OUT
 
@@ -42,8 +46,8 @@ def tile_multiheadattention_pa_t_kernel(
     nc = tc.nc
     with ExitStack() as ctx:
         const = ctx.enter_context(tc.tile_pool(name="const", bufs=1))
-        x_pool = ctx.enter_context(tc.tile_pool(name="x_pool", bufs=3))
-        inp_pool = ctx.enter_context(tc.tile_pool(name="inp_pool", bufs=5))
+        x_pool = ctx.enter_context(tc.tile_pool(name="x_pool", bufs=4))
+        inp_pool = ctx.enter_context(tc.tile_pool(name="inp_pool", bufs=6))
         front = ctx.enter_context(tc.tile_pool(name="front", bufs=3))
         back = ctx.enter_context(tc.tile_pool(name="back", bufs=4))
         small = ctx.enter_context(tc.tile_pool(name="small", bufs=4))
@@ -57,18 +61,21 @@ def tile_multiheadattention_pa_t_kernel(
         x_tiles = {}
         inp_tiles = {}
 
-        def load_chunk(c):
+        def load_x(c):
             x_sb = x_pool.tile([P, HEADS, ROWS, D_HEAD], BF16, name="x_sb")
             rows = x_view[:, c * CHUNK : (c + 1) * CHUNK, :].rearrange("h (p i) d -> p h (i d)", i=ROWS)
             for g in range(PASSES):
                 heads = slice(g * HEADS_PER_PASS, (g + 1) * HEADS_PER_PASS)
                 nc.sync.dma_start(out=x_sb[:, heads].rearrange("p h i d -> p h (i d)"), in_=rows[:, heads, :])
             x_tiles[c] = x_sb
+
+        def load_inp(c):
             inp_sb = inp_pool.tile([P, ROWS, N_OUT], BF16, name="inp_sb")
             nc.sync.dma_start(out=inp_sb[:].rearrange("p i n -> p (i n)"), in_=inp_view[c])
             inp_tiles[c] = inp_sb
 
-        load_chunk(0)
+        load_x(0)
+        load_x(1)
 
         w1 = const.tile([P, PASSES * 2 * N1], U8, align_bytes=64)
         w2 = const.tile([P, PASSES * 2 * N2], U8, align_bytes=64)
@@ -93,11 +100,27 @@ def tile_multiheadattention_pa_t_kernel(
                     in_=scales[:, 4 * quadrant : 4 * quadrant + 4, :].bitcast(I32).rearrange("g r n -> r g n"),
                 )
 
-        gain = const.tile([P, N_OUT], BF16)
-        bias = const.tile([P, N_OUT], BF16)
-        nc.sync.dma_start(out=gain[:], in_=ln_a.partition_broadcast(P))
-        nc.sync.dma_start(out=bias[:], in_=ln_b.partition_broadcast(P))
-        load_chunk(1)
+        gain_bias_row = const.tile([P, 2 * N_OUT], BF16)
+        nc.vector.memset(gain_bias_row[:], 0.0)
+        nc.scalar.dma_start(out=gain_bias_row[0:1, 0:N_OUT], in_=ln_a.rearrange("(o n) -> o n", o=1))
+        nc.scalar.dma_start(out=gain_bias_row[0:1, N_OUT : 2 * N_OUT], in_=ln_b.rearrange("(o n) -> o n", o=1))
+        load_inp(0)
+        load_inp(1)
+        ones = const.tile([P, P], BF16)
+        nc.vector.memset(ones[:], 1.0)
+        gain_bias = const.tile([P, 2 * N_OUT], BF16)
+        gain = gain_bias[:, 0:N_OUT]
+        bias = gain_bias[:, N_OUT : 2 * N_OUT]
+
+        def spread_gain_bias():
+            for first in range(0, 2 * N_OUT, BANK):
+                width = min(BANK, 2 * N_OUT - first)
+                spread = tp_pool.tile([P, BANK], F32, name="tp")
+                nc.tensor.matmul(
+                    out=spread[:, 0:width], lhsT=ones[:], rhs=gain_bias_row[:, first : first + width],
+                    start=True, stop=True,
+                )
+                nc.vector.tensor_copy(out=gain_bias[:, first : first + width], in_=spread[:, 0:width])
 
         ident = const.tile([P, P], F32)
         make_identity(nc, ident[:])
@@ -132,7 +155,7 @@ def tile_multiheadattention_pa_t_kernel(
             y_sb = front.tile([P, HALVES, PAIRS, HEADS, QUADS], F32, name="y_sb")
             for s in range(HALVES):
                 picked = words[:, :, i, s, :, :].rearrange("p h m u -> p u h m")
-                if s == 0:
+                if s == 0 and k % VECTOR_SORTS_EVERY == 0:
                     nc.vector.tensor_copy(out=y_sb[:, s], in_=picked)
                 else:
                     nc.scalar.copy(out=y_sb[:, s], in_=picked)
@@ -227,7 +250,7 @@ def tile_multiheadattention_pa_t_kernel(
         def centre(k):
             c_sb = back.tile([P, N_OUT], F32, name="cen_sb")
             nc.vector.scalar_tensor_tensor(
-                out=c_sb[:], in0=z.pop(k)[:], scalar=neg_mean.pop(k)[:, 0:1], in1=gain[:], op0=ALU.add, op1=ALU.mult
+                out=c_sb[:], in0=z.pop(k)[:], scalar=neg_mean.pop(k)[:, 0:1], in1=gain, op0=ALU.add, op1=ALU.mult
             )
             centred[k] = c_sb
 
@@ -250,7 +273,7 @@ def tile_multiheadattention_pa_t_kernel(
             c, i = divmod(k, ROWS)
             o_sb = back.tile([P, N_OUT], F32, name="o_sb")
             nc.vector.scalar_tensor_tensor(
-                out=o_sb[:], in0=centred.pop(k)[:], scalar=inv_sigma.pop(k)[:, 0:1], in1=bias[:],
+                out=o_sb[:], in0=centred.pop(k)[:], scalar=inv_sigma.pop(k)[:, 0:1], in1=bias,
                 op0=ALU.mult, op1=ALU.add,
             )
             nc.sync.dma_start(out=out_view[c][:, i, :], in_=o_sb[:])
@@ -262,10 +285,13 @@ def tile_multiheadattention_pa_t_kernel(
         with tc.manual_schedule():
             for step in range(N_TILES + 8):
                 if step % ROWS == 0 and step // ROWS + 2 < N_CHUNKS:
-                    load_chunk(step // ROWS + 2)
+                    load_x(step // ROWS + 2)
+                    load_inp(step // ROWS + 2)
                 run(project, step - 4)
                 run(add_residual, step - 5)
                 run(transpose_words, step - 1)
+                if step == SPREAD_STEP:
+                    spread_gain_bias()
                 run(group_words, step - 2)
                 run(add_eps, step - 7)
                 run(quantise, step - 3)
@@ -274,5 +300,5 @@ def tile_multiheadattention_pa_t_kernel(
                 run(centre, step - 6)
                 run(negate_mean, step - 5)
                 run(finish, step - 7)
-                run(sort_words, step)
                 run(root, step - 6)
+                run(sort_words, step)

@@ -22,7 +22,6 @@ N2 = 128
 N_OUT = N1 + N2
 EPS = 1e-3
 BANK = 512
-SPREAD_STEP = 2
 
 HALVES = 2
 PASSES = 2
@@ -35,7 +34,8 @@ CHUNK = P * ROWS
 N_CHUNKS = TOKENS // CHUNK
 N_TILES = TOKENS // P
 
-VECTOR_SORTS_EVERY = 4
+CV = 384
+WG = N_OUT - CV
 
 FLOPS = 2 * TOKENS * (HEADS * 64) * N_OUT
 
@@ -49,10 +49,13 @@ def tile_multiheadattention_pa_t_kernel(
         x_pool = ctx.enter_context(tc.tile_pool(name="x_pool", bufs=4))
         inp_pool = ctx.enter_context(tc.tile_pool(name="inp_pool", bufs=6))
         front = ctx.enter_context(tc.tile_pool(name="front", bufs=3))
+        z_pool = ctx.enter_context(tc.tile_pool(name="z_pool", bufs=5))
         back = ctx.enter_context(tc.tile_pool(name="back", bufs=4))
-        small = ctx.enter_context(tc.tile_pool(name="small", bufs=4))
-        tp_pool = ctx.enter_context(tc.psum_pool(name="tp_pool", bufs=4))
+        junk = ctx.enter_context(tc.tile_pool(name="junk", bufs=2))
+        small = ctx.enter_context(tc.tile_pool(name="small", bufs=6))
+        tp_pool = ctx.enter_context(tc.psum_pool(name="tp_pool", bufs=3))
         y_pool = ctx.enter_context(tc.psum_pool(name="y_pool", bufs=2))
+        gb_pool = ctx.enter_context(tc.psum_pool(name="gb_pool", bufs=1))
 
         x_view = attn_out.rearrange("h b l d -> h (b l) d")
         inp_view = inp.rearrange("(c p i) n -> c p (i n)", p=P, i=ROWS)
@@ -102,25 +105,35 @@ def tile_multiheadattention_pa_t_kernel(
 
         gain_bias_row = const.tile([P, 2 * N_OUT], BF16)
         nc.vector.memset(gain_bias_row[:], 0.0)
-        nc.scalar.dma_start(out=gain_bias_row[0:1, 0:N_OUT], in_=ln_a.rearrange("(o n) -> o n", o=1))
-        nc.scalar.dma_start(out=gain_bias_row[0:1, N_OUT : 2 * N_OUT], in_=ln_b.rearrange("(o n) -> o n", o=1))
+        a_row = ln_a.rearrange("(o n) -> o n", o=1)
+        b_row = ln_b.rearrange("(o n) -> o n", o=1)
+        nc.scalar.dma_start(out=gain_bias_row[0:1, 0:CV], in_=a_row[:, 0:CV])
+        nc.scalar.dma_start(out=gain_bias_row[0:1, CV : 2 * CV], in_=b_row[:, 0:CV])
+        nc.scalar.dma_start(out=gain_bias_row[0:1, 2 * CV : 2 * CV + WG], in_=a_row[:, CV:N_OUT])
+        nc.scalar.dma_start(out=gain_bias_row[0:1, 2 * CV + WG : 2 * N_OUT], in_=b_row[:, CV:N_OUT])
         load_inp(0)
         load_inp(1)
         ones = const.tile([P, P], BF16)
         nc.vector.memset(ones[:], 1.0)
-        gain_bias = const.tile([P, 2 * N_OUT], BF16)
-        gain = gain_bias[:, 0:N_OUT]
-        bias = gain_bias[:, N_OUT : 2 * N_OUT]
+        gb_ps = gb_pool.tile([P, 2 * CV], BF16, name="gb_ps")
+        gain_v = gb_ps[:, 0:CV]
+        bias_v = gb_ps[:, CV : 2 * CV]
+        gb_g = const.tile([P, 2 * WG], BF16)
+        gain_g = gb_g[:, 0:WG]
+        bias_g = gb_g[:, WG : 2 * WG]
 
         def spread_gain_bias():
-            for first in range(0, 2 * N_OUT, BANK):
-                width = min(BANK, 2 * N_OUT - first)
-                spread = tp_pool.tile([P, BANK], F32, name="tp")
+            for first in (0, CV):
                 nc.tensor.matmul(
-                    out=spread[:, 0:width], lhsT=ones[:], rhs=gain_bias_row[:, first : first + width],
+                    out=gb_ps[:, first : first + CV], lhsT=ones[:], rhs=gain_bias_row[:, first : first + CV],
                     start=True, stop=True,
                 )
-                nc.vector.tensor_copy(out=gain_bias[:, first : first + width], in_=spread[:, 0:width])
+            spread = tp_pool.tile([P, BANK], F32, name="tp")
+            nc.tensor.matmul(
+                out=spread[:, 0 : 2 * WG], lhsT=ones[:], rhs=gain_bias_row[:, 2 * CV : 2 * N_OUT],
+                start=True, stop=True,
+            )
+            return spread
 
         ident = const.tile([P, P], F32)
         make_identity(nc, ident[:])
@@ -143,6 +156,7 @@ def tile_multiheadattention_pa_t_kernel(
         sigma_eps = {}
         centred = {}
         inv_sigma = {}
+        results = {}
 
         def sort_words(k):
             c, i = divmod(k, ROWS)
@@ -153,37 +167,30 @@ def tile_multiheadattention_pa_t_kernel(
                 .rearrange("p (h i s m u) -> p h i s m u", h=HEADS, i=ROWS, s=HALVES, m=QUADS, u=PAIRS)
             )
             y_sb = front.tile([P, HALVES, PAIRS, HEADS, QUADS], F32, name="y_sb")
-            for s in range(HALVES):
-                picked = words[:, :, i, s, :, :].rearrange("p h m u -> p u h m")
-                if s == 0 and k % VECTOR_SORTS_EVERY == 0:
-                    nc.vector.tensor_copy(out=y_sb[:, s], in_=picked)
-                else:
-                    nc.scalar.copy(out=y_sb[:, s], in_=picked)
+            nc.vector.tensor_copy(out=y_sb[:, 0], in_=words[:, :, i, 0, :, :].rearrange("p h m u -> p u h m"))
+            nc.scalar.copy(out=y_sb[:, 1], in_=words[:, :, i, 1, :, :].rearrange("p h m u -> p u h m"))
             sorted_words[k] = y_sb
 
-        def transpose_words(k):
-            y_sb = sorted_words.pop(k)
-            banks = []
-            for s in range(HALVES):
-                tp = tp_pool.tile([P, PASSES, PAIRS, P], F32, name="tp")
-                for g in range(PASSES):
-                    heads = slice(g * HEADS_PER_PASS, (g + 1) * HEADS_PER_PASS)
-                    for u in range(PAIRS):
-                        nc.tensor.transpose(
-                            tp[:, g, u, :], y_sb[:, s, u, heads, :].rearrange("p h m -> p (h m)"), ident[:]
-                        )
-                banks.append(tp)
-            transposed[k] = banks
+        def transpose_words(k, s):
+            y_sb = sorted_words[k]
+            tp = tp_pool.tile([P, PASSES, PAIRS, P], F32, name="tp")
+            for g in range(PASSES):
+                heads = slice(g * HEADS_PER_PASS, (g + 1) * HEADS_PER_PASS)
+                for u in range(PAIRS):
+                    nc.tensor.transpose(
+                        tp[:, g, u, :], y_sb[:, s, u, heads, :].rearrange("p h m -> p (h m)"), ident[:]
+                    )
+            transposed[(k, s)] = tp
 
-        def group_words(k):
-            banks = transposed.pop(k)
-            g_sb = front.tile([P, HALVES, PASSES * P * 4], BF16, name="g_sb", align_bytes=64)
-            for s in range(HALVES):
-                nc.scalar.copy(
-                    out=g_sb[:, s, :].bitcast(F32).rearrange("p (g t u) -> p g t u", g=PASSES, u=PAIRS),
-                    in_=banks[s][:].rearrange("p g u t -> p g t u"),
-                )
-            grouped[k] = g_sb
+        def group_words(k, s):
+            if s == 0:
+                g_new = front.tile([P, HALVES, PASSES * P * 4], BF16, name="g_sb", align_bytes=64)
+                grouped[k] = g_new
+            g_sb = grouped[k]
+            nc.scalar.copy(
+                out=g_sb[:, s, :].bitcast(F32).rearrange("p (g t u) -> p g t u", g=PASSES, u=PAIRS),
+                in_=transposed.pop((k, s))[:].rearrange("p g u t -> p g t u"),
+            )
 
         def quantise(k):
             g_sb = grouped.pop(k)
@@ -217,7 +224,7 @@ def tile_multiheadattention_pa_t_kernel(
 
         def add_residual(k):
             c, i = divmod(k, ROWS)
-            z_sb = back.tile([P, N_OUT], F32, name="z_sb")
+            z_sb = z_pool.tile([P, N_OUT], F32, name="z_sb")
             sums = small.tile([P, 2], F32, name="sums")
             nc.vector.scalar_tensor_tensor(
                 out=z_sb[:, 0:N1], in0=y1.pop(k)[:], scalar=1.0, in1=inp_tiles[c][:, i, 0:N1],
@@ -239,7 +246,7 @@ def tile_multiheadattention_pa_t_kernel(
             neg_mean[k] = nm
 
         def sum_squares(k):
-            squares = back.tile([P, N_OUT], BF16, name="squares")
+            squares = junk.tile([P, N_OUT], BF16, name="squares")
             ssq = small.tile([P, 1], F32, name="ssq")
             nc.scalar.activation(
                 out=squares[:], in_=z[k][:], func=ACT.Square, bias=neg_mean[k][:, 0:1], scale=1.0,
@@ -248,9 +255,9 @@ def tile_multiheadattention_pa_t_kernel(
             square_sums[k] = ssq
 
         def centre(k):
-            c_sb = back.tile([P, N_OUT], F32, name="cen_sb")
+            c_sb = back.tile([P, CV], F32, name="cen_sb")
             nc.vector.scalar_tensor_tensor(
-                out=c_sb[:], in0=z.pop(k)[:], scalar=neg_mean.pop(k)[:, 0:1], in1=gain, op0=ALU.add, op1=ALU.mult
+                out=c_sb[:], in0=z[k][:, 0:CV], scalar=neg_mean[k][:, 0:1], in1=gain_v, op0=ALU.add, op1=ALU.mult
             )
             centred[k] = c_sb
 
@@ -269,36 +276,54 @@ def tile_multiheadattention_pa_t_kernel(
             nc.vector.reciprocal(out=inv[:], in_=sigma_eps.pop(k)[:])
             inv_sigma[k] = inv
 
-        def finish(k):
-            c, i = divmod(k, ROWS)
+        def normalise_rest(k):
             o_sb = back.tile([P, N_OUT], F32, name="o_sb")
+            rest = o_sb[:, CV:N_OUT]
+            nc.gpsimd.tensor_scalar(
+                out=rest, in0=z.pop(k)[:, CV:N_OUT], scalar1=neg_mean.pop(k)[:, 0:1], scalar2=inv_sigma[k][:, 0:1],
+                op0=ALU.add, op1=ALU.mult,
+            )
+            nc.gpsimd.tensor_tensor(out=rest, in0=rest, in1=gain_g, op=ALU.mult)
+            nc.gpsimd.tensor_tensor(out=rest, in0=rest, in1=bias_g, op=ALU.add)
+            results[k] = o_sb
+
+        def finish(k):
             nc.vector.scalar_tensor_tensor(
-                out=o_sb[:], in0=centred.pop(k)[:], scalar=inv_sigma.pop(k)[:, 0:1], in1=bias,
+                out=results[k][:, 0:CV], in0=centred.pop(k)[:], scalar=inv_sigma.pop(k)[:, 0:1], in1=bias_v,
                 op0=ALU.mult, op1=ALU.add,
             )
-            nc.sync.dma_start(out=out_view[c][:, i, :], in_=o_sb[:])
 
-        def run(stage, k):
+        def store(k):
+            c, i = divmod(k, ROWS)
+            nc.sync.dma_start(out=out_view[c][:, i, :], in_=results.pop(k)[:])
+
+        def run(stage, k, *more):
             if 0 <= k < N_TILES:
-                stage(k)
+                stage(k, *more)
 
         with tc.manual_schedule():
-            for step in range(N_TILES + 8):
+            for step in range(N_TILES + 9):
                 if step % ROWS == 0 and step // ROWS + 2 < N_CHUNKS:
                     load_x(step // ROWS + 2)
                     load_inp(step // ROWS + 2)
+                if step == 0:
+                    spread_ps = spread_gain_bias()
+                if step == 1:
+                    nc.vector.tensor_copy(out=gb_g[:], in_=spread_ps[:, 0 : 2 * WG])
+                run(normalise_rest, step - 8)
+                run(transpose_words, step - 1, 0)
+                run(group_words, step - 2, 0)
                 run(project, step - 4)
+                run(transpose_words, step - 1, 1)
+                run(group_words, step - 2, 1)
                 run(add_residual, step - 5)
-                run(transpose_words, step - 1)
-                if step == SPREAD_STEP:
-                    spread_gain_bias()
-                run(group_words, step - 2)
-                run(add_eps, step - 7)
-                run(quantise, step - 3)
-                run(invert, step - 7)
                 run(sum_squares, step - 6)
                 run(centre, step - 6)
+                run(finish, step - 8)
                 run(negate_mean, step - 5)
-                run(finish, step - 7)
-                run(root, step - 6)
+                run(add_eps, step - 7)
                 run(sort_words, step)
+                run(root, step - 6)
+                run(quantise, step - 3)
+                run(invert, step - 7)
+                run(store, step - 8)

@@ -34,7 +34,7 @@ CHUNK = P * ROWS
 N_CHUNKS = TOKENS // CHUNK
 N_TILES = TOKENS // P
 
-CV = 384
+CV = 448
 WG = N_OUT - CV
 
 FLOPS = 2 * TOKENS * (HEADS * 64) * N_OUT
@@ -167,7 +167,10 @@ def tile_multiheadattention_pa_t_kernel(
                 .rearrange("p (h i s m u) -> p h i s m u", h=HEADS, i=ROWS, s=HALVES, m=QUADS, u=PAIRS)
             )
             y_sb = front.tile([P, HALVES, PAIRS, HEADS, QUADS], F32, name="y_sb")
-            nc.vector.tensor_copy(out=y_sb[:, 0], in_=words[:, :, i, 0, :, :].rearrange("p h m u -> p u h m"))
+            if k % 4 != 3:
+                nc.vector.tensor_copy(out=y_sb[:, 0], in_=words[:, :, i, 0, :, :].rearrange("p h m u -> p u h m"))
+            else:
+                nc.scalar.copy(out=y_sb[:, 0], in_=words[:, :, i, 0, :, :].rearrange("p h m u -> p u h m"))
             nc.scalar.copy(out=y_sb[:, 1], in_=words[:, :, i, 1, :, :].rearrange("p h m u -> p u h m"))
             sorted_words[k] = y_sb
 

@@ -35,6 +35,8 @@ N_CHUNKS = TOKENS // CHUNK
 N_TILES = TOKENS // P
 
 CV = 448
+SPREAD_STEP = 2
+TAIL_TILES = 3
 WG = N_OUT - CV
 
 FLOPS = 2 * TOKENS * (HEADS * 64) * N_OUT
@@ -128,12 +130,12 @@ def tile_multiheadattention_pa_t_kernel(
                     out=gb_ps[:, first : first + CV], lhsT=ones[:], rhs=gain_bias_row[:, first : first + CV],
                     start=True, stop=True,
                 )
-            spread = tp_pool.tile([P, BANK], F32, name="tp")
+            spread = y_pool.tile([P, N1], F32, name="y1_ps")
             nc.tensor.matmul(
                 out=spread[:, 0 : 2 * WG], lhsT=ones[:], rhs=gain_bias_row[:, 2 * CV : 2 * N_OUT],
                 start=True, stop=True,
             )
-            return spread
+            nc.vector.tensor_copy(out=gb_g[:], in_=spread[:, 0 : 2 * WG])
 
         ident = const.tile([P, P], F32)
         make_identity(nc, ident[:])
@@ -258,10 +260,15 @@ def tile_multiheadattention_pa_t_kernel(
             square_sums[k] = ssq
 
         def centre(k):
-            c_sb = back.tile([P, CV], F32, name="cen_sb")
+            c_sb = back.tile([P, N_OUT], F32, name="cen_sb")
             nc.vector.scalar_tensor_tensor(
-                out=c_sb[:], in0=z[k][:, 0:CV], scalar=neg_mean[k][:, 0:1], in1=gain_v, op0=ALU.add, op1=ALU.mult
+                out=c_sb[:, 0:CV], in0=z[k][:, 0:CV], scalar=neg_mean[k][:, 0:1], in1=gain_v, op0=ALU.add, op1=ALU.mult
             )
+            if k >= N_TILES - TAIL_TILES:
+                nc.vector.scalar_tensor_tensor(
+                    out=c_sb[:, CV:N_OUT], in0=z[k][:, CV:N_OUT], scalar=neg_mean[k][:, 0:1], in1=gain_g,
+                    op0=ALU.add, op1=ALU.mult,
+                )
             centred[k] = c_sb
 
         def root(k):
@@ -271,7 +278,7 @@ def tile_multiheadattention_pa_t_kernel(
 
         def add_eps(k):
             se = small.tile([P, 1], F32, name="se")
-            nc.vector.tensor_scalar_add(out=se[:], in0=sigma.pop(k)[:], scalar1=EPS)
+            nc.scalar.activation(out=se[:], in_=sigma.pop(k)[:], func=ACT.Identity, bias=EPS, scale=1.0)
             sigma_eps[k] = se
 
         def invert(k):
@@ -281,6 +288,9 @@ def tile_multiheadattention_pa_t_kernel(
 
         def normalise_rest(k):
             o_sb = back.tile([P, N_OUT], F32, name="o_sb")
+            results[k] = o_sb
+            if k >= N_TILES - TAIL_TILES:
+                return
             rest = o_sb[:, CV:N_OUT]
             nc.gpsimd.tensor_scalar(
                 out=rest, in0=z.pop(k)[:, CV:N_OUT], scalar1=neg_mean.pop(k)[:, 0:1], scalar2=inv_sigma[k][:, 0:1],
@@ -288,13 +298,17 @@ def tile_multiheadattention_pa_t_kernel(
             )
             nc.gpsimd.tensor_tensor(out=rest, in0=rest, in1=gain_g, op=ALU.mult)
             nc.gpsimd.tensor_tensor(out=rest, in0=rest, in1=bias_g, op=ALU.add)
-            results[k] = o_sb
 
         def finish(k):
             nc.vector.scalar_tensor_tensor(
-                out=results[k][:, 0:CV], in0=centred.pop(k)[:], scalar=inv_sigma.pop(k)[:, 0:1], in1=bias_v,
+                out=results[k][:, 0:CV], in0=centred[k][:, 0:CV], scalar=inv_sigma[k][:, 0:1], in1=bias_v,
                 op0=ALU.mult, op1=ALU.add,
             )
+            if k >= N_TILES - TAIL_TILES:
+                nc.vector.scalar_tensor_tensor(
+                    out=results[k][:, CV:N_OUT], in0=centred[k][:, CV:N_OUT], scalar=inv_sigma[k][:, 0:1], in1=bias_g,
+                    op0=ALU.mult, op1=ALU.add,
+                )
 
         def store(k):
             c, i = divmod(k, ROWS)
@@ -309,22 +323,20 @@ def tile_multiheadattention_pa_t_kernel(
                 if step % ROWS == 0 and step // ROWS + 2 < N_CHUNKS:
                     load_x(step // ROWS + 2)
                     load_inp(step // ROWS + 2)
-                if step == 0:
-                    spread_ps = spread_gain_bias()
-                if step == 1:
-                    nc.vector.tensor_copy(out=gb_g[:], in_=spread_ps[:, 0 : 2 * WG])
                 run(normalise_rest, step - 8)
                 run(transpose_words, step - 1, 0)
                 run(group_words, step - 2, 0)
                 run(project, step - 4)
                 run(transpose_words, step - 1, 1)
                 run(group_words, step - 2, 1)
+                if step == SPREAD_STEP:
+                    spread_gain_bias()
                 run(add_residual, step - 5)
                 run(sum_squares, step - 6)
+                run(add_eps, step - 7)
                 run(centre, step - 6)
                 run(finish, step - 8)
                 run(negate_mean, step - 5)
-                run(add_eps, step - 7)
                 run(sort_words, step)
                 run(root, step - 6)
                 run(quantise, step - 3)

@@ -169,7 +169,7 @@ def tile_multiheadattention_pa_t_kernel(
                 .rearrange("p (h i s m u) -> p h i s m u", h=HEADS, i=ROWS, s=HALVES, m=QUADS, u=PAIRS)
             )
             y_sb = front.tile([P, HALVES, PAIRS, HEADS, QUADS], F32, name="y_sb")
-            if k % 4 != 3:
+            if k % 8 in (0, 1, 2, 4, 5):
                 nc.vector.tensor_copy(out=y_sb[:, 0], in_=words[:, :, i, 0, :, :].rearrange("p h m u -> p u h m"))
             else:
                 nc.scalar.copy(out=y_sb[:, 0], in_=words[:, :, i, 0, :, :].rearrange("p h m u -> p u h m"))

@@ -49,10 +49,11 @@ def tile_multiheadattention_pa_t_kernel(
     with ExitStack() as ctx:
         const = ctx.enter_context(tc.tile_pool(name="const", bufs=1))
         x_pool = ctx.enter_context(tc.tile_pool(name="x_pool", bufs=4))
-        inp_pool = ctx.enter_context(tc.tile_pool(name="inp_pool", bufs=6))
+        inp_pool = ctx.enter_context(tc.tile_pool(name="inp_pool", bufs=7))
         front = ctx.enter_context(tc.tile_pool(name="front", bufs=3))
         z_pool = ctx.enter_context(tc.tile_pool(name="z_pool", bufs=5))
         back = ctx.enter_context(tc.tile_pool(name="back", bufs=4))
+        out_pool = ctx.enter_context(tc.tile_pool(name="out_pool", bufs=8))
         junk = ctx.enter_context(tc.tile_pool(name="junk", bufs=2))
         small = ctx.enter_context(tc.tile_pool(name="small", bufs=6))
         tp_pool = ctx.enter_context(tc.psum_pool(name="tp_pool", bufs=3))
@@ -97,6 +98,8 @@ def tile_multiheadattention_pa_t_kernel(
             in_=w_proj2_words.bitcast(I32).rearrange("g p n -> p g n"),
         )
         for quadrant in range(4):
+            if quadrant == 2:
+                load_x(2)
             for plane, scales in ((w1_scl, w_proj1_scales), (w2_scl, w_proj2_scales)):
                 nc.sync.dma_start(
                     out=plane[32 * quadrant : 32 * quadrant + 4, :]
@@ -114,6 +117,8 @@ def tile_multiheadattention_pa_t_kernel(
         nc.scalar.dma_start(out=gain_bias_row[0:1, 2 * CV : 2 * CV + WG], in_=a_row[:, CV:N_OUT])
         nc.scalar.dma_start(out=gain_bias_row[0:1, 2 * CV + WG : 2 * N_OUT], in_=b_row[:, CV:N_OUT])
         load_inp(0)
+        for c in range(3, 3):
+            load_x(c)
         load_inp(1)
         ones = const.tile([P, P], BF16)
         nc.vector.memset(ones[:], 1.0)
@@ -287,7 +292,7 @@ def tile_multiheadattention_pa_t_kernel(
             inv_sigma[k] = inv
 
         def normalise_rest(k):
-            o_sb = back.tile([P, N_OUT], F32, name="o_sb")
+            o_sb = out_pool.tile([P, N_OUT], F32, name="o_sb")
             results[k] = o_sb
             if k >= N_TILES - TAIL_TILES:
                 return
@@ -320,8 +325,9 @@ def tile_multiheadattention_pa_t_kernel(
 
         with tc.manual_schedule():
             for step in range(N_TILES + 9):
+                if step % ROWS == 0 and step // ROWS + 3 < N_CHUNKS:
+                    load_x(step // ROWS + 3)
                 if step % ROWS == 0 and step // ROWS + 2 < N_CHUNKS:
-                    load_x(step // ROWS + 2)
                     load_inp(step // ROWS + 2)
                 run(normalise_rest, step - 8)
                 run(transpose_words, step - 1, 0)

@@ -36,7 +36,7 @@ N_TILES = TOKENS // P
 
 CV = 448
 SPREAD_STEP = 2
-TAIL_TILES = 3
+TAIL_TILES = 4
 WG = N_OUT - CV
 
 FLOPS = 2 * TOKENS * (HEADS * 64) * N_OUT
@@ -53,7 +53,7 @@ def tile_multiheadattention_pa_t_kernel(
         front = ctx.enter_context(tc.tile_pool(name="front", bufs=3))
         z_pool = ctx.enter_context(tc.tile_pool(name="z_pool", bufs=5))
         back = ctx.enter_context(tc.tile_pool(name="back", bufs=4))
-        out_pool = ctx.enter_context(tc.tile_pool(name="out_pool", bufs=8))
+        out_pool = ctx.enter_context(tc.tile_pool(name="out_pool", bufs=5))
         junk = ctx.enter_context(tc.tile_pool(name="junk", bufs=2))
         small = ctx.enter_context(tc.tile_pool(name="small", bufs=6))
         tp_pool = ctx.enter_context(tc.psum_pool(name="tp_pool", bufs=3))
@@ -117,8 +117,6 @@ def tile_multiheadattention_pa_t_kernel(
         nc.scalar.dma_start(out=gain_bias_row[0:1, 2 * CV : 2 * CV + WG], in_=a_row[:, CV:N_OUT])
         nc.scalar.dma_start(out=gain_bias_row[0:1, 2 * CV + WG : 2 * N_OUT], in_=b_row[:, CV:N_OUT])
         load_inp(0)
-        for c in range(3, 3):
-            load_x(c)
         load_inp(1)
         ones = const.tile([P, P], BF16)
         nc.vector.memset(ones[:], 1.0)
@@ -292,32 +290,47 @@ def tile_multiheadattention_pa_t_kernel(
             inv_sigma[k] = inv
 
         def normalise_rest(k):
-            o_sb = out_pool.tile([P, N_OUT], F32, name="o_sb")
-            results[k] = o_sb
+            if k % 2 == 0:
+                o_sb = out_pool.tile([P, 2, N_OUT], F32, name="o_sb")
+                results[k] = o_sb
+                results[k + 1] = o_sb
             if k >= N_TILES - TAIL_TILES:
                 return
-            rest = o_sb[:, CV:N_OUT]
             nc.gpsimd.tensor_scalar(
-                out=rest, in0=z.pop(k)[:, CV:N_OUT], scalar1=neg_mean.pop(k)[:, 0:1], scalar2=inv_sigma[k][:, 0:1],
-                op0=ALU.add, op1=ALU.mult,
+                out=results[k][:, k % 2, CV:N_OUT], in0=z.pop(k)[:, CV:N_OUT], scalar1=neg_mean.pop(k)[:, 0:1],
+                scalar2=inv_sigma[k][:, 0:1], op0=ALU.add, op1=ALU.mult,
             )
-            nc.gpsimd.tensor_tensor(out=rest, in0=rest, in1=gain_g, op=ALU.mult)
-            nc.gpsimd.tensor_tensor(out=rest, in0=rest, in1=bias_g, op=ALU.add)
+
+        def scale_rest(k, row, op):
+            if k % 2 == 0 or k >= N_TILES - TAIL_TILES:
+                return
+            rest = results[k][:, :, CV:N_OUT]
+            nc.gpsimd.tensor_tensor(
+                out=rest, in0=rest, in1=row.unsqueeze(1).to_broadcast([P, 2, WG]), op=op
+            )
 
         def finish(k):
             nc.vector.scalar_tensor_tensor(
-                out=results[k][:, 0:CV], in0=centred[k][:, 0:CV], scalar=inv_sigma[k][:, 0:1], in1=bias_v,
+                out=results[k][:, k % 2, 0:CV], in0=centred[k][:, 0:CV], scalar=inv_sigma[k][:, 0:1], in1=bias_v,
                 op0=ALU.mult, op1=ALU.add,
             )
             if k >= N_TILES - TAIL_TILES:
                 nc.vector.scalar_tensor_tensor(
-                    out=results[k][:, CV:N_OUT], in0=centred[k][:, CV:N_OUT], scalar=inv_sigma[k][:, 0:1], in1=bias_g,
+                    out=results[k][:, k % 2, CV:N_OUT], in0=centred[k][:, CV:N_OUT], scalar=inv_sigma[k][:, 0:1], in1=bias_g,
                     op0=ALU.mult, op1=ALU.add,
                 )
 
         def store(k):
             c, i = divmod(k, ROWS)
-            nc.sync.dma_start(out=out_view[c][:, i, :], in_=results.pop(k)[:])
+            nc.sync.dma_start(out=out_view[c][:, i, :], in_=results.pop(k)[:, k % 2, :])
+
+        def store_pair(k):
+            if k % 2 == 1 and k < N_TILES - TAIL_TILES:
+                pair = results.pop(k)
+                results.pop(k - 1)
+                nc.sync.dma_start(
+                    out=out_view[k // ROWS].rearrange("p i n -> p (i n)"), in_=pair[:].rearrange("p i n -> p (i n)")
+                )
 
         def run(stage, k, *more):
             if 0 <= k < N_TILES:
@@ -330,6 +343,8 @@ def tile_multiheadattention_pa_t_kernel(
                 if step % ROWS == 0 and step // ROWS + 2 < N_CHUNKS:
                     load_inp(step // ROWS + 2)
                 run(normalise_rest, step - 8)
+                run(scale_rest, step - 8, gain_g, ALU.mult)
+                run(scale_rest, step - 9, bias_g, ALU.add)
                 run(transpose_words, step - 1, 0)
                 run(group_words, step - 2, 0)
                 run(project, step - 4)
@@ -347,4 +362,6 @@ def tile_multiheadattention_pa_t_kernel(
                 run(root, step - 6)
                 run(quantise, step - 3)
                 run(invert, step - 7)
-                run(store, step - 8)
+                run(store_pair, step - 9)
+                if step - 8 >= N_TILES - TAIL_TILES:
+                    run(store, step - 8)

from contextlib import ExitStack

import concourse.mybir as mybir
from concourse.masks import make_identity

F32 = mybir.dt.float32
BF16 = mybir.dt.bfloat16
I32 = mybir.dt.int32
U32 = mybir.dt.uint32
U8 = mybir.dt.uint8
FP8X4 = mybir.dt.float8_e4m3fn_x4
FP4X4 = mybir.dt.float4_e2m1fn_x4
ALU = mybir.AluOpType
ACT = mybir.ActivationFunctionType

P = 128
HEADS = 16
D_HEAD = 128
TOKENS = 4096
N1 = 512
N2 = 128
N_OUT = N1 + N2
EPS = 1e-3
BANK = 512

HALVES = 2
PASSES = 2
HEADS_PER_PASS = HEADS // PASSES
QUADS = 16
PAIRS = 2

ROWS = 2
CHUNK = P * ROWS
N_CHUNKS = TOKENS // CHUNK
N_TILES = TOKENS // P

CV = 448
SPREAD_STEP = 2
TAIL_TILES = 4
WG = N_OUT - CV

FLOPS = 2 * TOKENS * (HEADS * 64) * N_OUT


def tile_multiheadattention_pa_t_kernel(
    tc, attn_out, inp, w_proj1_words, w_proj1_scales, w_proj2_words, w_proj2_scales, ln_a, ln_b, out
):
    nc = tc.nc
    with ExitStack() as ctx:
        const = ctx.enter_context(tc.tile_pool(name="const", bufs=1))
        x_pool = ctx.enter_context(tc.tile_pool(name="x_pool", bufs=4))
        inp_pool = ctx.enter_context(tc.tile_pool(name="inp_pool", bufs=7))
        front = ctx.enter_context(tc.tile_pool(name="front", bufs=3))
        z_pool = ctx.enter_context(tc.tile_pool(name="z_pool", bufs=5))
        back = ctx.enter_context(tc.tile_pool(name="back", bufs=4))
        out_pool = ctx.enter_context(tc.tile_pool(name="out_pool", bufs=5))
        junk = ctx.enter_context(tc.tile_pool(name="junk", bufs=2))
        small = ctx.enter_context(tc.tile_pool(name="small", bufs=6))
        tp_pool = ctx.enter_context(tc.psum_pool(name="tp_pool", bufs=3))
        y_pool = ctx.enter_context(tc.psum_pool(name="y_pool", bufs=2))
        gb_pool = ctx.enter_context(tc.psum_pool(name="gb_pool", bufs=1))

        x_view = attn_out.rearrange("h b l d -> h (b l) d")
        inp_view = inp.rearrange("(c p i) n -> c p (i n)", p=P, i=ROWS)
        out_view = out.rearrange("(c p i) n -> c p i n", p=P, i=ROWS)

        x_tiles = {}
        inp_tiles = {}

        def load_x(c):
            x_sb = x_pool.tile([P, HEADS, ROWS, D_HEAD], BF16, name="x_sb")
            rows = x_view[:, c * CHUNK : (c + 1) * CHUNK, :].rearrange("h (p i) d -> p h (i d)", i=ROWS)
            for g in range(PASSES):
                heads = slice(g * HEADS_PER_PASS, (g + 1) * HEADS_PER_PASS)
                nc.sync.dma_start(out=x_sb[:, heads].rearrange("p h i d -> p h (i d)"), in_=rows[:, heads, :])
            x_tiles[c] = x_sb

        def load_inp(c):
            inp_sb = inp_pool.tile([P, ROWS, N_OUT], BF16, name="inp_sb")
            nc.sync.dma_start(out=inp_sb[:].rearrange("p i n -> p (i n)"), in_=inp_view[c])
            inp_tiles[c] = inp_sb

        load_x(0)
        load_x(1)

        w1 = const.tile([P, PASSES * 2 * N1], U8, align_bytes=64)
        w2 = const.tile([P, PASSES * 2 * N2], U8, align_bytes=64)
        w1_scl = const.tile([P, PASSES * N1], U8, align_bytes=64)
        w2_scl = const.tile([P, PASSES * N2], U8, align_bytes=64)
        nc.vector.memset(w1_scl[:].bitcast(I32), 0)
        nc.vector.memset(w2_scl[:].bitcast(I32), 0)
        nc.sync.dma_start(
            out=w1[:].bitcast(I32).rearrange("p (g n) -> p g n", g=PASSES),
            in_=w_proj1_words.bitcast(I32).rearrange("g p n -> p g n"),
        )
        nc.sync.dma_start(
            out=w2[:].bitcast(I32).rearrange("p (g n) -> p g n", g=PASSES),
            in_=w_proj2_words.bitcast(I32).rearrange("g p n -> p g n"),
        )
        for quadrant in range(4):
            if quadrant == 2:
                load_x(2)
            for plane, scales in ((w1_scl, w_proj1_scales), (w2_scl, w_proj2_scales)):
                nc.sync.dma_start(
                    out=plane[32 * quadrant : 32 * quadrant + 4, :]
                    .bitcast(I32)
                    .rearrange("r (g n) -> r g n", g=PASSES),
                    in_=scales[:, 4 * quadrant : 4 * quadrant + 4, :].bitcast(I32).rearrange("g r n -> r g n"),
                )

        gain_bias_row = const.tile([P, 2 * N_OUT], BF16)
        nc.vector.memset(gain_bias_row[:], 0.0)
        a_row = ln_a.rearrange("(o n) -> o n", o=1)
        b_row = ln_b.rearrange("(o n) -> o n", o=1)
        nc.scalar.dma_start(out=gain_bias_row[0:1, 0:CV], in_=a_row[:, 0:CV])
        nc.scalar.dma_start(out=gain_bias_row[0:1, CV : 2 * CV], in_=b_row[:, 0:CV])
        nc.scalar.dma_start(out=gain_bias_row[0:1, 2 * CV : 2 * CV + WG], in_=a_row[:, CV:N_OUT])
        nc.scalar.dma_start(out=gain_bias_row[0:1, 2 * CV + WG : 2 * N_OUT], in_=b_row[:, CV:N_OUT])
        load_inp(0)
        load_inp(1)
        ones = const.tile([P, P], BF16)
        nc.vector.memset(ones[:], 1.0)
        gb_ps = gb_pool.tile([P, 2 * CV], BF16, name="gb_ps")
        gain_v = gb_ps[:, 0:CV]
        bias_v = gb_ps[:, CV : 2 * CV]
        gb_g = const.tile([P, 2 * WG], BF16)
        gain_g = gb_g[:, 0:WG]
        bias_g = gb_g[:, WG : 2 * WG]

        def spread_gain_bias():
            for first in (0, CV):
                nc.tensor.matmul(
                    out=gb_ps[:, first : first + CV], lhsT=ones[:], rhs=gain_bias_row[:, first : first + CV],
                    start=True, stop=True,
                )
            spread = y_pool.tile([P, N1], F32, name="y1_ps")
            nc.tensor.matmul(
                out=spread[:, 0 : 2 * WG], lhsT=ones[:], rhs=gain_bias_row[:, 2 * CV : 2 * N_OUT],
                start=True, stop=True,
            )
            nc.vector.tensor_copy(out=gb_g[:], in_=spread[:, 0 : 2 * WG])

        ident = const.tile([P, P], F32)
        make_identity(nc, ident[:])
        one = const.tile([P, 1], F32)
        nc.vector.memset(one[:], 1.0)
        nc.scalar.activation(out=one[:], in_=one[:], func=ACT.Sqrt)

        sorted_words = {}
        transposed = {}
        grouped = {}
        codes = {}
        code_scales = {}
        y1 = {}
        y2 = {}
        z = {}
        row_sums = {}
        neg_mean = {}
        square_sums = {}
        sigma = {}
        sigma_eps = {}
        centred = {}
        inv_sigma = {}
        results = {}

        def sort_words(k):
            c, i = divmod(k, ROWS)
            words = (
                x_tiles[c][:]
                .rearrange("p h i d -> p (h i d)")
                .bitcast(F32)
                .rearrange("p (h i s m u) -> p h i s m u", h=HEADS, i=ROWS, s=HALVES, m=QUADS, u=PAIRS)
            )
            y_sb = front.tile([P, HALVES, PAIRS, HEADS, QUADS], F32, name="y_sb")
            if k % 8 in (0, 1, 2, 4, 5):
                nc.vector.tensor_copy(out=y_sb[:, 0], in_=words[:, :, i, 0, :, :].rearrange("p h m u -> p u h m"))
            else:
                nc.scalar.copy(out=y_sb[:, 0], in_=words[:, :, i, 0, :, :].rearrange("p h m u -> p u h m"))
            nc.scalar.copy(out=y_sb[:, 1], in_=words[:, :, i, 1, :, :].rearrange("p h m u -> p u h m"))
            sorted_words[k] = y_sb

        def transpose_words(k, s):
            y_sb = sorted_words[k]
            tp = tp_pool.tile([P, PASSES, PAIRS, P], F32, name="tp")
            for g in range(PASSES):
                heads = slice(g * HEADS_PER_PASS, (g + 1) * HEADS_PER_PASS)
                for u in range(PAIRS):
                    nc.tensor.transpose(
                        tp[:, g, u, :], y_sb[:, s, u, heads, :].rearrange("p h m -> p (h m)"), ident[:]
                    )
            transposed[(k, s)] = tp

        def group_words(k, s):
            if s == 0:
                g_new = front.tile([P, HALVES, PASSES * P * 4], BF16, name="g_sb", align_bytes=64)
                grouped[k] = g_new
            g_sb = grouped[k]
            nc.scalar.copy(
                out=g_sb[:, s, :].bitcast(F32).rearrange("p (g t u) -> p g t u", g=PASSES, u=PAIRS),
                in_=transposed.pop((k, s))[:].rearrange("p g u t -> p g t u"),
            )

        def quantise(k):
            g_sb = grouped.pop(k)
            c_sb = front.tile([P, HALVES * PASSES * P], U32, name="c_sb", align_bytes=64)
            s_sb = front.tile([P, HALVES * PASSES * P], U8, name="s_sb", align_bytes=64)
            nc.vector.quantize_mx(
                out=c_sb[:].bitcast(FP8X4), scales=s_sb[:], in_=g_sb[:].rearrange("p s e -> p (s e)")
            )
            codes[k] = c_sb
            code_scales[k] = s_sb

        def project(k):
            c_sb = codes.pop(k)
            s_sb = code_scales.pop(k)
            y1_ps = y_pool.tile([P, N1], F32, name="y1_ps")
            y2_ps = y_pool.tile([P, N2], F32, name="y2_ps")
            for s, (acc, w, w_scl, n) in enumerate(((y1_ps, w1, w1_scl, N1), (y2_ps, w2, w2_scl, N2))):
                for g in range(PASSES):
                    cols = slice((s * PASSES + g) * P, (s * PASSES + g + 1) * P)
                    nc.tensor.matmul_mx(
                        out=acc[:],
                        lhsT=c_sb[:, cols].bitcast(FP8X4),
                        lhsT_scale=s_sb[:, cols],
                        rhs=w[:, g * 2 * n : (g + 1) * 2 * n].bitcast(FP4X4),
                        rhs_scale=w_scl[:, g * n : (g + 1) * n],
                        start=(g == 0),
                        stop=(g == PASSES - 1),
                    )
            y1[k] = y1_ps
            y2[k] = y2_ps

        def add_residual(k):
            c, i = divmod(k, ROWS)
            z_sb = z_pool.tile([P, N_OUT], F32, name="z_sb")
            sums = small.tile([P, 2], F32, name="sums")
            nc.vector.scalar_tensor_tensor(
                out=z_sb[:, 0:N1], in0=y1.pop(k)[:], scalar=1.0, in1=inp_tiles[c][:, i, 0:N1],
                op0=ALU.mult, op1=ALU.add, accum_out=sums[:, 0:1],
            )
            nc.vector.scalar_tensor_tensor(
                out=z_sb[:, N1:N_OUT], in0=y2.pop(k)[:], scalar=1.0, in1=inp_tiles[c][:, i, N1:N_OUT],
                op0=ALU.mult, op1=ALU.add, accum_out=sums[:, 1:2],
            )
            z[k] = z_sb
            row_sums[k] = sums

        def negate_mean(k):
            sums = row_sums.pop(k)
            nm = small.tile([P, 1], F32, name="nm")
            nc.vector.tensor_scalar(
                out=nm[:], in0=sums[:, 0:1], scalar1=sums[:, 1:2], scalar2=-1.0 / N_OUT, op0=ALU.add, op1=ALU.mult
            )
            neg_mean[k] = nm

        def sum_squares(k):
            squares = junk.tile([P, N_OUT], BF16, name="squares")
            ssq = small.tile([P, 1], F32, name="ssq")
            nc.scalar.activation(
                out=squares[:], in_=z[k][:], func=ACT.Square, bias=neg_mean[k][:, 0:1], scale=1.0,
                accum_out=ssq[:, 0:1],
            )
            square_sums[k] = ssq

        def centre(k):
            c_sb = back.tile([P, N_OUT], F32, name="cen_sb")
            nc.vector.scalar_tensor_tensor(
                out=c_sb[:, 0:CV], in0=z[k][:, 0:CV], scalar=neg_mean[k][:, 0:1], in1=gain_v, op0=ALU.add, op1=ALU.mult
            )
            if k >= N_TILES - TAIL_TILES:
                nc.vector.scalar_tensor_tensor(
                    out=c_sb[:, CV:N_OUT], in0=z[k][:, CV:N_OUT], scalar=neg_mean[k][:, 0:1], in1=gain_g,
                    op0=ALU.add, op1=ALU.mult,
                )
            centred[k] = c_sb

        def root(k):
            sg = small.tile([P, 1], F32, name="sg")
            nc.scalar.activation(out=sg[:], in_=square_sums.pop(k)[:], func=ACT.Sqrt, scale=1.0 / (N_OUT - 1))
            sigma[k] = sg

        def add_eps(k):
            se = small.tile([P, 1], F32, name="se")
            nc.scalar.activation(out=se[:], in_=sigma.pop(k)[:], func=ACT.Identity, bias=EPS, scale=1.0)
            sigma_eps[k] = se

        def invert(k):
            inv = small.tile([P, 1], F32, name="inv")
            nc.vector.reciprocal(out=inv[:], in_=sigma_eps.pop(k)[:])
            inv_sigma[k] = inv

        def normalise_rest(k):
            if k % 2 == 0:
                o_sb = out_pool.tile([P, 2, N_OUT], F32, name="o_sb")
                results[k] = o_sb
                results[k + 1] = o_sb
            if k >= N_TILES - TAIL_TILES:
                return
            nc.gpsimd.tensor_scalar(
                out=results[k][:, k % 2, CV:N_OUT], in0=z.pop(k)[:, CV:N_OUT], scalar1=neg_mean.pop(k)[:, 0:1],
                scalar2=inv_sigma[k][:, 0:1], op0=ALU.add, op1=ALU.mult,
            )

        def scale_rest(k, row, op):
            if k % 2 == 0 or k >= N_TILES - TAIL_TILES:
                return
            rest = results[k][:, :, CV:N_OUT]
            nc.gpsimd.tensor_tensor(
                out=rest, in0=rest, in1=row.unsqueeze(1).to_broadcast([P, 2, WG]), op=op
            )

        def finish(k):
            nc.vector.scalar_tensor_tensor(
                out=results[k][:, k % 2, 0:CV], in0=centred[k][:, 0:CV], scalar=inv_sigma[k][:, 0:1], in1=bias_v,
                op0=ALU.mult, op1=ALU.add,
            )
            if k >= N_TILES - TAIL_TILES:
                nc.vector.scalar_tensor_tensor(
                    out=results[k][:, k % 2, CV:N_OUT], in0=centred[k][:, CV:N_OUT], scalar=inv_sigma[k][:, 0:1], in1=bias_g,
                    op0=ALU.mult, op1=ALU.add,
                )

        def store(k):
            c, i = divmod(k, ROWS)
            nc.sync.dma_start(out=out_view[c][:, i, :], in_=results.pop(k)[:, k % 2, :])

        def store_pair(k):
            if k % 2 == 1 and k < N_TILES - TAIL_TILES:
                pair = results.pop(k)
                results.pop(k - 1)
                nc.sync.dma_start(
                    out=out_view[k // ROWS].rearrange("p i n -> p (i n)"), in_=pair[:].rearrange("p i n -> p (i n)")
                )

        def run(stage, k, *more):
            if 0 <= k < N_TILES:
                stage(k, *more)

        with tc.manual_schedule():
            for step in range(N_TILES + 9):
                if step % ROWS == 0 and step // ROWS + 3 < N_CHUNKS:
                    load_x(step // ROWS + 3)
                if step % ROWS == 0 and step // ROWS + 2 < N_CHUNKS:
                    load_inp(step // ROWS + 2)
                run(normalise_rest, step - 8)
                run(scale_rest, step - 8, gain_g, ALU.mult)
                run(scale_rest, step - 9, bias_g, ALU.add)
                run(transpose_words, step - 1, 0)
                run(group_words, step - 2, 0)
                run(project, step - 4)
                run(transpose_words, step - 1, 1)
                run(group_words, step - 2, 1)
                if step == SPREAD_STEP:
                    spread_gain_bias()
                run(add_residual, step - 5)
                run(sum_squares, step - 6)
                run(add_eps, step - 7)
                run(centre, step - 6)
                run(finish, step - 8)
                run(negate_mean, step - 5)
                run(sort_words, step)
                run(root, step - 6)
                run(quantise, step - 3)
                run(invert, step - 7)
                run(store_pair, step - 9)
                if step - 8 >= N_TILES - TAIL_TILES:
                    run(store, step - 8)
